import numpy as np
import ml_dtypes


def mxq(x, axis, fmt="e4m3"):
    dtype, down = {"e4m3": (ml_dtypes.float8_e4m3fn, 7), "e5m2": (ml_dtypes.float8_e5m2, 14)}[fmt]
    v = np.moveaxis(np.asarray(x, np.float32).astype(ml_dtypes.bfloat16).astype(np.float64), axis, -1)
    blocks = v.reshape(v.shape[:-1] + (-1, 32))
    amax = np.abs(blocks).max(-1, keepdims=True)
    byte = np.maximum(np.where(amax > 0, np.frexp(amax)[1] - 1 + 127, 0) - down, 1)
    scale = np.exp2(byte - 127.0)
    codes = (blocks / scale).astype(np.float32).astype(dtype).astype(np.float64)
    return np.moveaxis((codes * scale).reshape(v.shape), -1, axis)


WIDE = False


def mx_kscale(k):
    if not WIDE:
        return np.ones(k)
    levels = np.array([10, -10, 5, -5, 0])
    a = np.random.permutation(np.resize(levels, k // 512 * 4)).reshape(k // 512, 4)
    idx = np.arange(k)
    return np.exp2(a[idx // 512, idx % 128 // 32])


BF16 = ml_dtypes.bfloat16


def bf(x):
    return np.asarray(x, np.float32).astype(BF16)


def f64(x):
    return np.asarray(x).astype(np.float64)


E2M1 = np.array([0.0, 0.5, 1.0, 1.5, 2.0, 3.0, 4.0, 6.0, -0.0, -0.5, -1.0, -1.5, -2.0, -3.0, -4.0, -6.0])


def pack_weight(w, fmt):
    k, n = w.shape
    w = f64(bf(w)).reshape(k // 32, 32, n)
    amax = np.abs(w).max(1)
    if fmt == "e4m3":
        byte = np.frexp(amax)[1] - 1 + 127 - 7
    else:
        mant, ex = np.frexp(amax / 6.0)
        byte = np.where(mant > 0.5, ex, ex - 1) + 127
    byte = np.clip(np.where(amax > 0, byte, 1), 1, 254)
    scaled = (w * np.exp2(127.0 - byte)[:, None, :]).reshape(k, n).astype(np.float32)
    by_word = np.ascontiguousarray(scaled.reshape(k // 512, 128, 4, n).transpose(0, 1, 3, 2))
    if fmt == "e4m3":
        words = by_word.astype(ml_dtypes.float8_e4m3fn).view(np.uint8)
    else:
        c = by_word.astype(ml_dtypes.float4_e2m1fn).view(np.uint8) & 0xF
        words = c[..., 0::2] | (c[..., 1::2] << 4)
    return np.ascontiguousarray(words), np.ascontiguousarray(byte.astype(np.uint8).reshape(k // 512, 16, n))


def unpack_weight(words, scales, fmt):
    g, p, n, _ = words.shape
    if fmt == "e4m3":
        vals = np.ascontiguousarray(words).view(ml_dtypes.float8_e4m3fn).astype(np.float64)
    else:
        nib = np.empty((g, p, n, 4), np.uint8)
        nib[..., 0::2] = words & 0xF
        nib[..., 1::2] = words >> 4
        vals = E2M1[nib]
    vals = vals * np.repeat(np.exp2(scales.astype(np.float64) - 127.0), 8, axis=1)[..., None]
    return vals.transpose(0, 1, 3, 2).reshape(g * 512, n)

def pack4(w):
    words, scales = pack_weight(w, "e2m1")
    return words.reshape(words.shape[0], 128, -1), scales


def unpack4(words, scales):
    return unpack_weight(words.reshape(words.shape[0], 128, -1, 2), scales, "e2m1")


B, N, HID, H, D = 2, 64, 512, 16, 64


def apply_rope(t, rope):
    freqs = rope[:, 0, :]
    cos = np.repeat(freqs[:, 0::2], 2, axis=-1)[None, None]
    sin = np.repeat(freqs[:, 1::2], 2, axis=-1)[None, None]
    tr = t.reshape(*t.shape[:-1], -1, 2)
    t_real, t_imag = tr[..., 0], tr[..., 1]
    t_rot = np.stack([-t_imag, t_real], axis=-1).reshape(t.shape)
    return t * cos + t_rot * sin


def setup_inputs():
    s = mx_kscale(HID)
    x = bf(np.random.standard_normal((B, N, HID)) * s)
    rope = bf(np.random.uniform(size=(N, 1, D)))
    words, scales = pack4(np.random.standard_normal((HID, 3 * H * D)) * 1.5 / np.sqrt(HID) / s[:, None])
    return {"x": x,
            "rope": rope,
            "qkv_w_words": words,
            "qkv_w_scales": scales}


def reference(x, rope, qkv_w_words, qkv_w_scales):
    r = f64(rope)
    qkv = (mxq(f64(x), 2, "e4m3") @ unpack4(qkv_w_words, qkv_w_scales)).reshape(B, N, 3, H, D)
    q = np.transpose(qkv[:, :, 0], (0, 2, 1, 3))
    k = np.transpose(qkv[:, :, 1], (0, 2, 1, 3))
    v = np.transpose(qkv[:, :, 2], (0, 2, 1, 3))
    return apply_rope(q, r), apply_rope(k, r), v

@@ -1,0 +1,167 @@
+from contextlib import ExitStack
+
+import concourse.masks as masks
+import concourse.mybir as mybir
+
+F32 = mybir.dt.float32
+BF16 = mybir.dt.bfloat16
+I32 = mybir.dt.int32
+U32 = mybir.dt.uint32
+U8 = mybir.dt.uint8
+FP8X4 = mybir.dt.float8_e4m3fn_x4
+FP4X4 = mybir.dt.float4_e2m1fn_x4
+MULT = mybir.AluOpType.mult
+ADD = mybir.AluOpType.add
+
+BATCH, POSITIONS, HIDDEN, HEADS, HEAD_DIM = 2, 64, 512, 16, 64
+P = 128
+PAIRS = HEAD_DIM // 2
+BANK_COLS = 512
+BANK_HEADS = BANK_COLS // HEAD_DIM
+BANKS_PER_PART = HEADS // BANK_HEADS
+PART_COLS = HEADS * HEAD_DIM
+Q_PART, K_PART, V_PART = 0, 1, 2
+WORD_BYTES = 2
+SCALE_ROWS = HIDDEN // 32
+
+FLOPS = 2 * P * HIDDEN * 3 * PART_COLS
+
+
+def tile_attention_pa_s_kernel(
+    tc, x, rope, qkv_w_words, qkv_w_scales, out_0, out_1, out_2
+):
+    nc = tc.nc
+    outs = (out_0, out_1, out_2)
+
+    with ExitStack() as ctx:
+        ctx.enter_context(tc.manual_schedule())
+        keep = ctx.enter_context(tc.tile_pool(name="keep", bufs=1))
+        rope_work = ctx.enter_context(tc.tile_pool(name="rope_work", bufs=2 * BANKS_PER_PART))
+        v_work = ctx.enter_context(tc.tile_pool(name="v_work", bufs=BANKS_PER_PART))
+        psum_x = ctx.enter_context(tc.psum_pool(name="psum_x", bufs=1))
+        psum_acc = ctx.enter_context(tc.psum_pool(name="psum_acc", bufs=3 * BANKS_PER_PART))
+
+        w_scales = keep.tile([P, 3 * PART_COLS], U8, align_bytes=64)
+        nc.vector.memset(w_scales[:].bitcast(I32), 0)
+
+        x_sb = keep.tile([P, HIDDEN], BF16)
+        nc.sync.dma_start(out=x_sb[:], in_=x.rearrange("b n k -> n b k"))
+
+        rope_first = keep.tile([P, HEAD_DIM], BF16)
+        nc.scalar.dma_start(
+            out=rope_first[:], in_=rope.to_broadcast([POSITIONS, BATCH, HEAD_DIM])
+        )
+
+        w_words = keep.tile([P, 3 * PART_COLS * WORD_BYTES], U8, align_bytes=64)
+
+        def load_words(part):
+            byte_cols = slice(part * PART_COLS * WORD_BYTES, (part + 1) * PART_COLS * WORD_BYTES)
+            nc.sync.dma_start(
+                out=w_words[:, byte_cols].bitcast(I32),
+                in_=qkv_w_words[0, :, byte_cols].bitcast(I32),
+            )
+
+        load_words(Q_PART)
+        for quadrant in range(4):
+            nc.sync.dma_start(
+                out=w_scales[32 * quadrant : 32 * quadrant + 4, :].bitcast(I32),
+                in_=qkv_w_scales[0, 4 * quadrant : 4 * quadrant + 4, :].bitcast(I32),
+            )
+        load_words(V_PART)
+        load_words(K_PART)
+
+        identity = keep.tile([P, P], F32)
+        masks.make_identity(nc, identity[:])
+
+        rope_second = keep.tile([P, HEAD_DIM], BF16)
+        first_pairs = rope_first[:].rearrange("p (j r) -> p j r", r=2)
+        second_pairs = rope_second[:].rearrange("p (j r) -> p j r", r=2)
+        nc.gpsimd.tensor_scalar(
+            out=second_pairs[:, :, 0:1],
+            in0=first_pairs[:, :, 1:2],
+            scalar1=-1.0,
+            scalar2=0.0,
+            op0=MULT,
+            op1=ADD,
+        )
+        nc.gpsimd.tensor_copy(out=second_pairs[:, :, 1:2], in_=first_pairs[:, :, 0:1])
+
+        x_words = x_sb[:].bitcast(F32)
+        x_t = psum_x.tile([P, 2, P], F32)
+        for u in range(2):
+            nc.tensor.transpose(x_t[:, u, :], x_words[:, u : HIDDEN // 2 : 2], identity[:])
+        grouped = keep.tile([P, 4 * P], BF16, align_bytes=64)
+        nc.vector.tensor_copy(
+            out=grouped[:].bitcast(F32).rearrange("p (m u) -> p m u", u=2),
+            in_=x_t[:].rearrange("p u m -> p m u"),
+        )
+        x_codes = keep.tile([P, P], U32, align_bytes=64)
+        x_scales = keep.tile([P, P], U8, align_bytes=64)
+        nc.vector.quantize_mx(out=x_codes[:].bitcast(FP8X4), scales=x_scales[:], in_=grouped[:])
+
+        pass_order = []
+        for half in range(BANKS_PER_PART):
+            pass_order.extend([(Q_PART, half), (V_PART, half)])
+        for half in range(BANKS_PER_PART):
+            pass_order.append((K_PART, half))
+
+        banks = {}
+        for part, half in pass_order:
+            first_col = part * PART_COLS + half * BANK_COLS
+            acc = psum_acc.tile([P, BANK_COLS], F32)
+            nc.tensor.matmul_mx(
+                out=acc[:],
+                lhsT=x_codes[:].bitcast(FP8X4),
+                lhsT_scale=x_scales[:],
+                rhs=w_words[
+                    :, first_col * WORD_BYTES : (first_col + BANK_COLS) * WORD_BYTES
+                ].bitcast(FP4X4),
+                rhs_scale=w_scales[:, first_col : first_col + BANK_COLS],
+                start=True,
+                stop=True,
+            )
+            banks[(part, half)] = acc
+
+        def store(part, half, result):
+            heads = slice(half * BANK_HEADS, (half + 1) * BANK_HEADS)
+            for b, queue in enumerate((nc.sync, nc.scalar)):
+                queue.dma_start(
+                    out=outs[part][b, heads, :, :].rearrange("h n d -> n h d"),
+                    in_=result[b:P:BATCH, :].rearrange("p (h d) -> p h d", d=HEAD_DIM),
+                )
+
+        for half in range(BANKS_PER_PART):
+            v_sb = v_work.tile([P, BANK_COLS], F32)
+            nc.scalar.copy(out=v_sb[:], in_=banks[(V_PART, half)][:])
+            store(V_PART, half, v_sb)
+
+        pair_shape = [P, BANK_HEADS, PAIRS, 2]
+        table_first = first_pairs.unsqueeze(1).to_broadcast(pair_shape)
+        table_second = second_pairs.unsqueeze(1).to_broadcast(pair_shape)
+        for part in (Q_PART, K_PART):
+            for half in range(BANKS_PER_PART):
+                pairs = banks[(part, half)][:].rearrange(
+                    "p (h j r) -> p h j r", j=PAIRS, r=2
+                )
+                from_first = rope_work.tile(pair_shape, F32)
+                nc.vector.tensor_tensor(
+                    out=from_first[:],
+                    in0=pairs[:, :, :, 0:1].to_broadcast(pair_shape),
+                    in1=table_first,
+                    op=MULT,
+                )
+                from_second = rope_work.tile(pair_shape, F32)
+                nc.vector.tensor_tensor(
+                    out=from_second[:],
+                    in0=pairs[:, :, :, 1:2].to_broadcast(pair_shape),
+                    in1=table_second,
+                    op=MULT,
+                )
+                turned = rope_work.tile([P, BANK_COLS], F32)
+                nc.gpsimd.tensor_tensor(
+                    out=turned[:].rearrange("p (h j r) -> p h j r", j=PAIRS, r=2),
+                    in0=from_first[:],
+                    in1=from_second[:],
+                    op=ADD,
+                )
+                store(part, half, turned)

@@ -138,30 +138,29 @@ def tile_attention_pa_s_kernel(
         pair_shape = [P, BANK_HEADS, PAIRS, 2]
         table_first = first_pairs.unsqueeze(1).to_broadcast(pair_shape)
         table_second = second_pairs.unsqueeze(1).to_broadcast(pair_shape)
-        for part in (Q_PART, K_PART):
-            for half in range(BANKS_PER_PART):
-                pairs = banks[(part, half)][:].rearrange(
-                    "p (h j r) -> p h j r", j=PAIRS, r=2
-                )
-                from_first = rope_work.tile(pair_shape, F32)
-                nc.vector.tensor_tensor(
-                    out=from_first[:],
-                    in0=pairs[:, :, :, 0:1].to_broadcast(pair_shape),
-                    in1=table_first,
-                    op=MULT,
-                )
-                from_second = rope_work.tile(pair_shape, F32)
-                nc.vector.tensor_tensor(
-                    out=from_second[:],
-                    in0=pairs[:, :, :, 1:2].to_broadcast(pair_shape),
-                    in1=table_second,
-                    op=MULT,
-                )
-                turned = rope_work.tile([P, BANK_COLS], F32)
-                nc.gpsimd.tensor_tensor(
-                    out=turned[:].rearrange("p (h j r) -> p h j r", j=PAIRS, r=2),
-                    in0=from_first[:],
-                    in1=from_second[:],
-                    op=ADD,
-                )
-                store(part, half, turned)
+        rope_banks = [(part, half) for part in (Q_PART, K_PART) for half in range(BANKS_PER_PART)]
+        for part, half in rope_banks:
+            pairs = banks[(part, half)][:].rearrange("p (h j r) -> p h j r", j=PAIRS, r=2)
+            from_first = rope_work.tile(pair_shape, F32)
+            nc.vector.tensor_tensor(
+                out=from_first[:],
+                in0=pairs[:, :, :, 0:1].to_broadcast(pair_shape),
+                in1=table_first,
+                op=MULT,
+            )
+            from_second = rope_work.tile(pair_shape, F32)
+            nc.vector.tensor_tensor(
+                out=from_second[:],
+                in0=pairs[:, :, :, 1:2].to_broadcast(pair_shape),
+                in1=table_second,
+                op=MULT,
+            )
+            adder = nc.vector if (part, half) == rope_banks[-1] else nc.gpsimd
+            turned = rope_work.tile([P, BANK_COLS], F32)
+            adder.tensor_tensor(
+                out=turned[:].rearrange("p (h j r) -> p h j r", j=PAIRS, r=2),
+                in0=from_first[:],
+                in1=from_second[:],
+                op=ADD,
+            )
+            store(part, half, turned)

@@ -16,13 +16,14 @@ ADD = mybir.AluOpType.add
 BATCH, POSITIONS, HIDDEN, HEADS, HEAD_DIM = 2, 64, 512, 16, 64
 P = 128
 PAIRS = HEAD_DIM // 2
-BANK_COLS = 512
-BANK_HEADS = BANK_COLS // HEAD_DIM
-BANKS_PER_PART = HEADS // BANK_HEADS
+UNIT_HEADS = 4
+UNIT_COLS = UNIT_HEADS * HEAD_DIM
+UNITS_PER_PART = HEADS // UNIT_HEADS
 PART_COLS = HEADS * HEAD_DIM
 Q_PART, K_PART, V_PART = 0, 1, 2
 WORD_BYTES = 2
-SCALE_ROWS = HIDDEN // 32
+PSUM_BANKS = 8
+VECTOR_SUMS = 2
 
 FLOPS = 2 * P * HIDDEN * 3 * PART_COLS
 
@@ -36,10 +37,10 @@ def tile_attention_pa_s_kernel(
     with ExitStack() as ctx:
         ctx.enter_context(tc.manual_schedule())
         keep = ctx.enter_context(tc.tile_pool(name="keep", bufs=1))
-        rope_work = ctx.enter_context(tc.tile_pool(name="rope_work", bufs=2 * BANKS_PER_PART))
-        v_work = ctx.enter_context(tc.tile_pool(name="v_work", bufs=BANKS_PER_PART))
+        rope_work = ctx.enter_context(tc.tile_pool(name="rope_work", bufs=2 * UNITS_PER_PART))
+        v_work = ctx.enter_context(tc.tile_pool(name="v_work", bufs=UNITS_PER_PART))
         psum_x = ctx.enter_context(tc.psum_pool(name="psum_x", bufs=1))
-        psum_acc = ctx.enter_context(tc.psum_pool(name="psum_acc", bufs=3 * BANKS_PER_PART))
+        psum_acc = ctx.enter_context(tc.psum_pool(name="psum_acc", bufs=PSUM_BANKS - 1))
 
         w_scales = keep.tile([P, 3 * PART_COLS], U8, align_bytes=64)
         nc.vector.memset(w_scales[:].bitcast(I32), 0)
@@ -61,13 +62,13 @@ def tile_attention_pa_s_kernel(
                 in_=qkv_w_words[0, :, byte_cols].bitcast(I32),
             )
 
-        load_words(Q_PART)
+        load_words(V_PART)
         for quadrant in range(4):
             nc.sync.dma_start(
                 out=w_scales[32 * quadrant : 32 * quadrant + 4, :].bitcast(I32),
                 in_=qkv_w_scales[0, 4 * quadrant : 4 * quadrant + 4, :].bitcast(I32),
             )
-        load_words(V_PART)
+        load_words(Q_PART)
         load_words(K_PART)
 
         identity = keep.tile([P, P], F32)
@@ -100,47 +101,47 @@ def tile_attention_pa_s_kernel(
         nc.vector.quantize_mx(out=x_codes[:].bitcast(FP8X4), scales=x_scales[:], in_=grouped[:])
 
         pass_order = []
-        for half in range(BANKS_PER_PART):
-            pass_order.extend([(Q_PART, half), (V_PART, half)])
-        for half in range(BANKS_PER_PART):
-            pass_order.append((K_PART, half))
+        for group in range(UNITS_PER_PART):
+            pass_order.extend([(V_PART, group), (Q_PART, group)])
+        for group in range(UNITS_PER_PART):
+            pass_order.append((K_PART, group))
 
-        banks = {}
-        for part, half in pass_order:
-            first_col = part * PART_COLS + half * BANK_COLS
-            acc = psum_acc.tile([P, BANK_COLS], F32)
+        sums = {}
+        for part, group in pass_order:
+            first_col = part * PART_COLS + group * UNIT_COLS
+            acc = psum_acc.tile([P, UNIT_COLS], F32)
             nc.tensor.matmul_mx(
                 out=acc[:],
                 lhsT=x_codes[:].bitcast(FP8X4),
                 lhsT_scale=x_scales[:],
                 rhs=w_words[
-                    :, first_col * WORD_BYTES : (first_col + BANK_COLS) * WORD_BYTES
+                    :, first_col * WORD_BYTES : (first_col + UNIT_COLS) * WORD_BYTES
                 ].bitcast(FP4X4),
-                rhs_scale=w_scales[:, first_col : first_col + BANK_COLS],
+                rhs_scale=w_scales[:, first_col : first_col + UNIT_COLS],
                 start=True,
                 stop=True,
             )
-            banks[(part, half)] = acc
+            sums[(part, group)] = acc
 
-        def store(part, half, result):
-            heads = slice(half * BANK_HEADS, (half + 1) * BANK_HEADS)
+        def store(part, group, result):
+            heads = slice(group * UNIT_HEADS, (group + 1) * UNIT_HEADS)
             for b, queue in enumerate((nc.sync, nc.scalar)):
                 queue.dma_start(
                     out=outs[part][b, heads, :, :].rearrange("h n d -> n h d"),
                     in_=result[b:P:BATCH, :].rearrange("p (h d) -> p h d", d=HEAD_DIM),
                 )
 
-        for half in range(BANKS_PER_PART):
-            v_sb = v_work.tile([P, BANK_COLS], F32)
-            nc.scalar.copy(out=v_sb[:], in_=banks[(V_PART, half)][:])
-            store(V_PART, half, v_sb)
+        for group in range(UNITS_PER_PART):
+            v_sb = v_work.tile([P, UNIT_COLS], F32)
+            nc.scalar.copy(out=v_sb[:], in_=sums[(V_PART, group)][:])
+            store(V_PART, group, v_sb)
 
-        pair_shape = [P, BANK_HEADS, PAIRS, 2]
+        pair_shape = [P, UNIT_HEADS, PAIRS, 2]
         table_first = first_pairs.unsqueeze(1).to_broadcast(pair_shape)
         table_second = second_pairs.unsqueeze(1).to_broadcast(pair_shape)
-        rope_banks = [(part, half) for part in (Q_PART, K_PART) for half in range(BANKS_PER_PART)]
-        for part, half in rope_banks:
-            pairs = banks[(part, half)][:].rearrange("p (h j r) -> p h j r", j=PAIRS, r=2)
+        rope_units = [(part, group) for part in (Q_PART, K_PART) for group in range(UNITS_PER_PART)]
+        for index, (part, group) in enumerate(rope_units):
+            pairs = sums[(part, group)][:].rearrange("p (h j r) -> p h j r", j=PAIRS, r=2)
             from_first = rope_work.tile(pair_shape, F32)
             nc.vector.tensor_tensor(
                 out=from_first[:],
@@ -155,12 +156,12 @@ def tile_attention_pa_s_kernel(
                 in1=table_second,
                 op=MULT,
             )
-            adder = nc.vector if (part, half) == rope_banks[-1] else nc.gpsimd
-            turned = rope_work.tile([P, BANK_COLS], F32)
+            adder = nc.gpsimd if index < len(rope_units) - VECTOR_SUMS else nc.vector
+            turned = rope_work.tile([P, UNIT_COLS], F32)
             adder.tensor_tensor(
                 out=turned[:].rearrange("p (h j r) -> p h j r", j=PAIRS, r=2),
                 in0=from_first[:],
                 in1=from_second[:],
                 op=ADD,
             )
-            store(part, half, turned)
+            store(part, group, turned)

@@ -125,8 +125,8 @@ def tile_attention_pa_s_kernel(
 
         def store(part, group, result):
             heads = slice(group * UNIT_HEADS, (group + 1) * UNIT_HEADS)
-            for b, queue in enumerate((nc.sync, nc.scalar)):
-                queue.dma_start(
+            for b in range(BATCH):
+                nc.sync.dma_start(
                     out=outs[part][b, heads, :, :].rearrange("h n d -> n h d"),
                     in_=result[b:P:BATCH, :].rearrange("p (h d) -> p h d", d=HEAD_DIM),
                 )

@@ -62,12 +62,12 @@ def tile_attention_pa_s_kernel(
                 in_=qkv_w_words[0, :, byte_cols].bitcast(I32),
             )
 
-        load_words(V_PART)
         for quadrant in range(4):
             nc.sync.dma_start(
                 out=w_scales[32 * quadrant : 32 * quadrant + 4, :].bitcast(I32),
                 in_=qkv_w_scales[0, 4 * quadrant : 4 * quadrant + 4, :].bitcast(I32),
             )
+        load_words(V_PART)
         load_words(Q_PART)
         load_words(K_PART)
 

@@ -48,9 +48,9 @@ def tile_attention_pa_s_kernel(
         x_sb = keep.tile([P, HIDDEN], BF16)
         nc.sync.dma_start(out=x_sb[:], in_=x.rearrange("b n k -> n b k"))
 
-        rope_first = keep.tile([P, HEAD_DIM], BF16)
+        tables = keep.tile([P, 2, HEAD_DIM], BF16)
         nc.scalar.dma_start(
-            out=rope_first[:], in_=rope.to_broadcast([POSITIONS, BATCH, HEAD_DIM])
+            out=tables[:, 0, :], in_=rope.to_broadcast([POSITIONS, BATCH, HEAD_DIM])
         )
 
         w_words = keep.tile([P, 3 * PART_COLS * WORD_BYTES], U8, align_bytes=64)
@@ -74,9 +74,8 @@ def tile_attention_pa_s_kernel(
         identity = keep.tile([P, P], F32)
         masks.make_identity(nc, identity[:])
 
-        rope_second = keep.tile([P, HEAD_DIM], BF16)
-        first_pairs = rope_first[:].rearrange("p (j r) -> p j r", r=2)
-        second_pairs = rope_second[:].rearrange("p (j r) -> p j r", r=2)
+        first_pairs = tables[:, 0, :].rearrange("p (j r) -> p j r", r=2)
+        second_pairs = tables[:, 1, :].rearrange("p (j r) -> p j r", r=2)
         nc.gpsimd.tensor_scalar(
             out=second_pairs[:, :, 0:1],
             in0=first_pairs[:, :, 1:2],
@@ -136,32 +135,29 @@ def tile_attention_pa_s_kernel(
             nc.scalar.copy(out=v_sb[:], in_=sums[(V_PART, group)][:])
             store(V_PART, group, v_sb)
 
-        pair_shape = [P, UNIT_HEADS, PAIRS, 2]
-        table_first = first_pairs.unsqueeze(1).to_broadcast(pair_shape)
-        table_second = second_pairs.unsqueeze(1).to_broadcast(pair_shape)
+        product_shape = [P, 2, UNIT_HEADS, PAIRS, 2]
+        both_tables = (
+            tables[:]
+            .rearrange("p s (j r) -> p s j r", r=2)
+            .unsqueeze(2)
+            .to_broadcast(product_shape)
+        )
         rope_units = [(part, group) for part in (Q_PART, K_PART) for group in range(UNITS_PER_PART)]
         for index, (part, group) in enumerate(rope_units):
-            pairs = sums[(part, group)][:].rearrange("p (h j r) -> p h j r", j=PAIRS, r=2)
-            from_first = rope_work.tile(pair_shape, F32)
-            nc.vector.tensor_tensor(
-                out=from_first[:],
-                in0=pairs[:, :, :, 0:1].to_broadcast(pair_shape),
-                in1=table_first,
-                op=MULT,
+            elements = (
+                sums[(part, group)][:]
+                .rearrange("p (h j s) -> p s h j", j=PAIRS, s=2)
+                .unsqueeze(4)
+                .to_broadcast(product_shape)
             )
-            from_second = rope_work.tile(pair_shape, F32)
-            nc.vector.tensor_tensor(
-                out=from_second[:],
-                in0=pairs[:, :, :, 1:2].to_broadcast(pair_shape),
-                in1=table_second,
-                op=MULT,
-            )
+            products = rope_work.tile(product_shape, F32)
+            nc.vector.tensor_tensor(out=products[:], in0=elements, in1=both_tables, op=MULT)
             adder = nc.gpsimd if index < len(rope_units) - VECTOR_SUMS else nc.vector
             turned = rope_work.tile([P, UNIT_COLS], F32)
             adder.tensor_tensor(
                 out=turned[:].rearrange("p (h j r) -> p h j r", j=PAIRS, r=2),
-                in0=from_first[:],
-                in1=from_second[:],
+                in0=products[:, 0],
+                in1=products[:, 1],
                 op=ADD,
             )
             store(part, group, turned)

@@ -16,14 +16,21 @@ ADD = mybir.AluOpType.add
 BATCH, POSITIONS, HIDDEN, HEADS, HEAD_DIM = 2, 64, 512, 16, 64
 P = 128
 PAIRS = HEAD_DIM // 2
-UNIT_HEADS = 4
-UNIT_COLS = UNIT_HEADS * HEAD_DIM
-UNITS_PER_PART = HEADS // UNIT_HEADS
+ROW_TOKENS = 2
+ROWS = POSITIONS // ROW_TOKENS
+HALVES = 2
+HALF_HEADS = HEADS // HALVES
+UNIT_HEADS = 2
+PASS_COLS = UNIT_HEADS * HEAD_DIM
+UNIT_COLS = ROW_TOKENS * PASS_COLS
+UNITS_PER_PART = HALF_HEADS // UNIT_HEADS
 PART_COLS = HEADS * HEAD_DIM
 Q_PART, K_PART, V_PART = 0, 1, 2
 WORD_BYTES = 2
 PSUM_BANKS = 8
 VECTOR_SUMS = 2
+BLOCK = ROWS
+PACK = 4
 
 FLOPS = 2 * P * HIDDEN * 3 * PART_COLS
 
@@ -46,11 +53,14 @@ def tile_attention_pa_s_kernel(
         nc.vector.memset(w_scales[:].bitcast(I32), 0)
 
         x_sb = keep.tile([P, HIDDEN], BF16)
-        nc.sync.dma_start(out=x_sb[:], in_=x.rearrange("b n k -> n b k"))
+        nc.sync.dma_start(out=x_sb[:], in_=x.rearrange("b n k -> (b n) k"))
 
-        tables = keep.tile([P, 2, HEAD_DIM], BF16)
+        tables = keep.tile([P, 2, ROW_TOKENS, HEAD_DIM], BF16)
         nc.scalar.dma_start(
-            out=tables[:, 0, :], in_=rope.to_broadcast([POSITIONS, BATCH, HEAD_DIM])
+            out=tables[:, 0].rearrange("p e d -> p (e d)"),
+            in_=rope.rearrange("(m e) o d -> m (e o d)", e=ROW_TOKENS)
+            .unsqueeze(0)
+            .to_broadcast([BATCH * HALVES, ROWS, ROW_TOKENS * HEAD_DIM]),
         )
 
         w_words = keep.tile([P, 3 * PART_COLS * WORD_BYTES], U8, align_bytes=64)
@@ -74,30 +84,44 @@ def tile_attention_pa_s_kernel(
         identity = keep.tile([P, P], F32)
         masks.make_identity(nc, identity[:])
 
-        first_pairs = tables[:, 0, :].rearrange("p (j r) -> p j r", r=2)
-        second_pairs = tables[:, 1, :].rearrange("p (j r) -> p j r", r=2)
+        first_pairs = tables[:, 0].rearrange("p e (j r) -> p e j r", r=2)
+        second_pairs = tables[:, 1].rearrange("p e (j r) -> p e j r", r=2)
         nc.gpsimd.tensor_scalar(
-            out=second_pairs[:, :, 0:1],
-            in0=first_pairs[:, :, 1:2],
+            out=second_pairs[:, :, :, 0:1],
+            in0=first_pairs[:, :, :, 1:2],
             scalar1=-1.0,
             scalar2=0.0,
             op0=MULT,
             op1=ADD,
         )
-        nc.gpsimd.tensor_copy(out=second_pairs[:, :, 1:2], in_=first_pairs[:, :, 0:1])
+        nc.gpsimd.tensor_copy(out=second_pairs[:, :, :, 1:2], in_=first_pairs[:, :, :, 0:1])
+
+        strip = keep.tile([P, 9 * BLOCK * PACK], BF16, align_bytes=64)
+        nc.vector.memset(strip[:].bitcast(I32), 0)
 
         x_words = x_sb[:].bitcast(F32)
         x_t = psum_x.tile([P, 2, P], F32)
         for u in range(2):
             nc.tensor.transpose(x_t[:, u, :], x_words[:, u : HIDDEN // 2 : 2], identity[:])
-        grouped = keep.tile([P, 4 * P], BF16, align_bytes=64)
         nc.vector.tensor_copy(
-            out=grouped[:].bitcast(F32).rearrange("p (m u) -> p m u", u=2),
-            in_=x_t[:].rearrange("p u m -> p m u"),
+            out=strip[:, BLOCK * PACK :]
+            .bitcast(F32)
+            .rearrange("p (e b z m u) -> p e b z m u", e=2, b=2, z=2, u=2)[:, :, :, 0],
+            in_=x_t[:].rearrange("p u (b m e) -> p e b m u", b=2, e=2),
         )
-        x_codes = keep.tile([P, P], U32, align_bytes=64)
-        x_scales = keep.tile([P, P], U8, align_bytes=64)
-        nc.vector.quantize_mx(out=x_codes[:].bitcast(FP8X4), scales=x_scales[:], in_=grouped[:])
+        x_codes = {}
+        x_scales = {}
+        for half in (1, 0):
+            codes = keep.tile([P, ROW_TOKENS * P], U32, align_bytes=64, name="codes%d" % half)
+            planes = keep.tile([P, ROW_TOKENS * P], U8, align_bytes=64, name="planes%d" % half)
+            first = (1 - half) * BLOCK * PACK
+            nc.vector.quantize_mx(
+                out=codes[:].bitcast(FP8X4),
+                scales=planes[:],
+                in_=strip[:, first : first + ROW_TOKENS * P * PACK],
+            )
+            x_codes[half] = codes
+            x_scales[half] = planes
 
         pass_order = []
         for group in range(UNITS_PER_PART):
@@ -107,57 +131,63 @@ def tile_attention_pa_s_kernel(
 
         sums = {}
         for part, group in pass_order:
-            first_col = part * PART_COLS + group * UNIT_COLS
             acc = psum_acc.tile([P, UNIT_COLS], F32)
-            nc.tensor.matmul_mx(
-                out=acc[:],
-                lhsT=x_codes[:].bitcast(FP8X4),
-                lhsT_scale=x_scales[:],
-                rhs=w_words[
-                    :, first_col * WORD_BYTES : (first_col + UNIT_COLS) * WORD_BYTES
-                ].bitcast(FP4X4),
-                rhs_scale=w_scales[:, first_col : first_col + UNIT_COLS],
-                start=True,
-                stop=True,
-            )
+            for e in range(ROW_TOKENS):
+                for half in (1, 0):
+                    first_col = part * PART_COLS + (half * HALF_HEADS + group * UNIT_HEADS) * HEAD_DIM
+                    nc.tensor.matmul_mx(
+                        out=acc[:, e * PASS_COLS : (e + 1) * PASS_COLS],
+                        lhsT=x_codes[half][:, e * P : (e + 1) * P].bitcast(FP8X4),
+                        lhsT_scale=x_scales[half][:, e * P : (e + 1) * P],
+                        rhs=w_words[
+                            :, first_col * WORD_BYTES : (first_col + PASS_COLS) * WORD_BYTES
+                        ].bitcast(FP4X4),
+                        rhs_scale=w_scales[:, first_col : first_col + PASS_COLS],
+                        start=(half == 1),
+                        stop=(half == 0),
+                    )
             sums[(part, group)] = acc
 
         def store(part, group, result):
-            heads = slice(group * UNIT_HEADS, (group + 1) * UNIT_HEADS)
-            for b in range(BATCH):
-                nc.sync.dma_start(
-                    out=outs[part][b, heads, :, :].rearrange("h n d -> n h d"),
-                    in_=result[b:P:BATCH, :].rearrange("p (h d) -> p h d", d=HEAD_DIM),
-                )
+            by_slot = outs[part].rearrange(
+                "b (g s) (m e) d -> s (b g) m (e d)", g=HALVES, e=ROW_TOKENS
+            )
+            for h in range(UNIT_HEADS):
+                nc.sync.dma_start(out=by_slot[group * UNIT_HEADS + h], in_=result[:, h, :])
 
         for group in range(UNITS_PER_PART):
-            v_sb = v_work.tile([P, UNIT_COLS], F32)
-            nc.scalar.copy(out=v_sb[:], in_=sums[(V_PART, group)][:])
+            v_sb = v_work.tile([P, UNIT_HEADS, ROW_TOKENS * HEAD_DIM], F32)
+            nc.scalar.copy(
+                out=v_sb[:].rearrange("p h (e d) -> p h e d", e=ROW_TOKENS),
+                in_=sums[(V_PART, group)][:].rearrange(
+                    "p (e h d) -> p h e d", e=ROW_TOKENS, h=UNIT_HEADS
+                ),
+            )
             store(V_PART, group, v_sb)
 
-        product_shape = [P, 2, UNIT_HEADS, PAIRS, 2]
+        product_shape = [P, 2, ROW_TOKENS, UNIT_HEADS, PAIRS, 2]
         both_tables = (
             tables[:]
-            .rearrange("p s (j r) -> p s j r", r=2)
-            .unsqueeze(2)
+            .rearrange("p s e (j r) -> p s e j r", r=2)
+            .unsqueeze(3)
             .to_broadcast(product_shape)
         )
         rope_units = [(part, group) for part in (Q_PART, K_PART) for group in range(UNITS_PER_PART)]
         for index, (part, group) in enumerate(rope_units):
             elements = (
                 sums[(part, group)][:]
-                .rearrange("p (h j s) -> p s h j", j=PAIRS, s=2)
-                .unsqueeze(4)
+                .rearrange("p (e h j s) -> p s e h j", e=ROW_TOKENS, h=UNIT_HEADS, s=2)
+                .unsqueeze(5)
                 .to_broadcast(product_shape)
             )
             products = rope_work.tile(product_shape, F32)
             nc.vector.tensor_tensor(out=products[:], in0=elements, in1=both_tables, op=MULT)
             adder = nc.gpsimd if index < len(rope_units) - VECTOR_SUMS else nc.vector
-            turned = rope_work.tile([P, UNIT_COLS], F32)
+            turned = rope_work.tile([P, UNIT_HEADS, ROW_TOKENS * HEAD_DIM], F32)
             adder.tensor_tensor(
-                out=turned[:].rearrange("p (h j r) -> p h j r", j=PAIRS, r=2),
-                in0=products[:, 0],
-                in1=products[:, 1],
+                out=turned[:].rearrange("p h (e d) -> p h e d", e=ROW_TOKENS),
+                in0=products[:, 0].rearrange("p e h j r -> p h e (j r)"),
+                in1=products[:, 1].rearrange("p e h j r -> p h e (j r)"),
                 op=ADD,
             )
             store(part, group, turned)

@@ -19,17 +19,15 @@ PAIRS = HEAD_DIM // 2
 ROW_TOKENS = 2
 ROWS = POSITIONS // ROW_TOKENS
 HALVES = 2
-HALF_HEADS = HEADS // HALVES
 UNIT_HEADS = 2
 PASS_COLS = UNIT_HEADS * HEAD_DIM
 UNIT_COLS = ROW_TOKENS * PASS_COLS
-UNITS_PER_PART = HALF_HEADS // UNIT_HEADS
+UNITS_PER_PART = HEADS // (HALVES * UNIT_HEADS)
 PART_COLS = HEADS * HEAD_DIM
 Q_PART, K_PART, V_PART = 0, 1, 2
 WORD_BYTES = 2
 PSUM_BANKS = 8
 VECTOR_SUMS = 2
-BLOCK = ROWS
 PACK = 4
 
 FLOPS = 2 * P * HIDDEN * 3 * PART_COLS
@@ -53,14 +51,14 @@ def tile_attention_pa_s_kernel(
         nc.vector.memset(w_scales[:].bitcast(I32), 0)
 
         x_sb = keep.tile([P, HIDDEN], BF16)
-        nc.sync.dma_start(out=x_sb[:], in_=x.rearrange("b n k -> (b n) k"))
+        nc.sync.dma_start(out=x_sb[:], in_=x.rearrange("b n k -> n b k"))
 
         tables = keep.tile([P, 2, ROW_TOKENS, HEAD_DIM], BF16)
         nc.scalar.dma_start(
             out=tables[:, 0].rearrange("p e d -> p (e d)"),
-            in_=rope.rearrange("(m e) o d -> m (e o d)", e=ROW_TOKENS)
-            .unsqueeze(0)
-            .to_broadcast([BATCH * HALVES, ROWS, ROW_TOKENS * HEAD_DIM]),
+            in_=rope.rearrange("(m e) o d -> m o (e d)", e=ROW_TOKENS).to_broadcast(
+                [ROWS, BATCH * HALVES, ROW_TOKENS * HEAD_DIM]
+            ),
         )
 
         w_words = keep.tile([P, 3 * PART_COLS * WORD_BYTES], U8, align_bytes=64)
@@ -96,32 +94,41 @@ def tile_attention_pa_s_kernel(
         )
         nc.gpsimd.tensor_copy(out=second_pairs[:, :, :, 1:2], in_=first_pairs[:, :, :, 0:1])
 
-        strip = keep.tile([P, 9 * BLOCK * PACK], BF16, align_bytes=64)
-        nc.vector.memset(strip[:].bitcast(I32), 0)
+        strips = []
+        for e in range(ROW_TOKENS):
+            strip = keep.tile([P, HALVES * P * PACK + 64], BF16, align_bytes=64, name="strip%d" % e)
+            nc.vector.memset(strip[:].bitcast(I32), 0)
+            strips.append(strip)
 
         x_words = x_sb[:].bitcast(F32)
         x_t = psum_x.tile([P, 2, P], F32)
         for u in range(2):
             nc.tensor.transpose(x_t[:, u, :], x_words[:, u : HIDDEN // 2 : 2], identity[:])
-        nc.vector.tensor_copy(
-            out=strip[:, BLOCK * PACK :]
-            .bitcast(F32)
-            .rearrange("p (e b z m u) -> p e b z m u", e=2, b=2, z=2, u=2)[:, :, :, 0],
-            in_=x_t[:].rearrange("p u (b m e) -> p e b m u", b=2, e=2),
-        )
-        x_codes = {}
-        x_scales = {}
-        for half in (1, 0):
-            codes = keep.tile([P, ROW_TOKENS * P], U32, align_bytes=64, name="codes%d" % half)
-            planes = keep.tile([P, ROW_TOKENS * P], U8, align_bytes=64, name="planes%d" % half)
-            first = (1 - half) * BLOCK * PACK
+        copiers = (nc.vector.tensor_copy, nc.scalar.copy)
+        for e in range(ROW_TOKENS):
+            copiers[e](
+                out=strips[e][:, 0 : 2 * 2 * (P + 2) * 2]
+                .bitcast(F32)
+                .rearrange("p (a y) -> p a y", a=HALVES)[:, :, 0 : 2 * P]
+                .rearrange("p a (m r) -> p a m r", r=8)[:, :, :, 0:4]
+                .rearrange("p a m (b u) -> p a m b u", u=2),
+                in_=x_t[:]
+                .rearrange("p u (m e b) -> p e m b u", e=2, b=2)[:, e]
+                .unsqueeze(1)
+                .to_broadcast([P, HALVES, ROWS, 2, 2]),
+            )
+        x_codes = []
+        x_scales = []
+        for e in range(ROW_TOKENS):
+            codes = keep.tile([P, HALVES * P], U32, align_bytes=64, name="codes%d" % e)
+            planes = keep.tile([P, HALVES * P], U8, align_bytes=64, name="planes%d" % e)
             nc.vector.quantize_mx(
                 out=codes[:].bitcast(FP8X4),
                 scales=planes[:],
-                in_=strip[:, first : first + ROW_TOKENS * P * PACK],
+                in_=strips[e][:, 0 : HALVES * P * PACK],
             )
-            x_codes[half] = codes
-            x_scales[half] = planes
+            x_codes.append(codes)
+            x_scales.append(planes)
 
         pass_order = []
         for group in range(UNITS_PER_PART):
@@ -134,11 +141,11 @@ def tile_attention_pa_s_kernel(
             acc = psum_acc.tile([P, UNIT_COLS], F32)
             for e in range(ROW_TOKENS):
                 for half in (1, 0):
-                    first_col = part * PART_COLS + (half * HALF_HEADS + group * UNIT_HEADS) * HEAD_DIM
+                    first_col = part * PART_COLS + (group * HALVES + half) * PASS_COLS
                     nc.tensor.matmul_mx(
                         out=acc[:, e * PASS_COLS : (e + 1) * PASS_COLS],
-                        lhsT=x_codes[half][:, e * P : (e + 1) * P].bitcast(FP8X4),
-                        lhsT_scale=x_scales[half][:, e * P : (e + 1) * P],
+                        lhsT=x_codes[e][:, half * P : (half + 1) * P].bitcast(FP8X4),
+                        lhsT_scale=x_scales[e][:, half * P : (half + 1) * P],
                         rhs=w_words[
                             :, first_col * WORD_BYTES : (first_col + PASS_COLS) * WORD_BYTES
                         ].bitcast(FP4X4),
@@ -149,11 +156,12 @@ def tile_attention_pa_s_kernel(
             sums[(part, group)] = acc
 
         def store(part, group, result):
-            by_slot = outs[part].rearrange(
-                "b (g s) (m e) d -> s (b g) m (e d)", g=HALVES, e=ROW_TOKENS
-            )
-            for h in range(UNIT_HEADS):
-                nc.sync.dma_start(out=by_slot[group * UNIT_HEADS + h], in_=result[:, h, :])
+            heads = slice(group * HALVES * UNIT_HEADS, (group + 1) * HALVES * UNIT_HEADS)
+            for b in range(BATCH):
+                nc.sync.dma_start(
+                    out=outs[part][b, heads, :, :].rearrange("x (m e) d -> m x (e d)", e=ROW_TOKENS),
+                    in_=result[b:P:BATCH, :, :],
+                )
 
         for group in range(UNITS_PER_PART):
             v_sb = v_work.tile([P, UNIT_HEADS, ROW_TOKENS * HEAD_DIM], F32)

@@ -23,6 +23,8 @@ UNIT_HEADS = 2
 PASS_COLS = UNIT_HEADS * HEAD_DIM
 UNIT_COLS = ROW_TOKENS * PASS_COLS
 UNITS_PER_PART = HEADS // (HALVES * UNIT_HEADS)
+STORE_UNITS = 2
+STORE_HEADS = STORE_UNITS * HALVES * UNIT_HEADS
 PART_COLS = HEADS * HEAD_DIM
 Q_PART, K_PART, V_PART = 0, 1, 2
 WORD_BYTES = 2
@@ -43,12 +45,14 @@ def tile_attention_pa_s_kernel(
         ctx.enter_context(tc.manual_schedule())
         keep = ctx.enter_context(tc.tile_pool(name="keep", bufs=1))
         rope_work = ctx.enter_context(tc.tile_pool(name="rope_work", bufs=2 * UNITS_PER_PART))
-        v_work = ctx.enter_context(tc.tile_pool(name="v_work", bufs=UNITS_PER_PART))
+        results = ctx.enter_context(tc.tile_pool(name="results", bufs=3 * UNITS_PER_PART // STORE_UNITS))
         psum_x = ctx.enter_context(tc.psum_pool(name="psum_x", bufs=1))
         psum_acc = ctx.enter_context(tc.psum_pool(name="psum_acc", bufs=PSUM_BANKS - 1))
 
         w_scales = keep.tile([P, 3 * PART_COLS], U8, align_bytes=64)
-        nc.vector.memset(w_scales[:].bitcast(I32), 0)
+        half_plane = 3 * PART_COLS // 2
+        nc.vector.memset(w_scales[:, 0:half_plane].bitcast(I32), 0)
+        nc.gpsimd.memset(w_scales[:, half_plane:].bitcast(F32), 0.0)
 
         x_sb = keep.tile([P, HIDDEN], BF16)
         nc.sync.dma_start(out=x_sb[:], in_=x.rearrange("b n k -> n b k"))
@@ -70,13 +74,13 @@ def tile_attention_pa_s_kernel(
                 in_=qkv_w_words[0, :, byte_cols].bitcast(I32),
             )
 
+        load_words(Q_PART)
         for quadrant in range(4):
             nc.sync.dma_start(
                 out=w_scales[32 * quadrant : 32 * quadrant + 4, :].bitcast(I32),
                 in_=qkv_w_scales[0, 4 * quadrant : 4 * quadrant + 4, :].bitcast(I32),
             )
         load_words(V_PART)
-        load_words(Q_PART)
         load_words(K_PART)
 
         identity = keep.tile([P, P], F32)
@@ -104,9 +108,8 @@ def tile_attention_pa_s_kernel(
         x_t = psum_x.tile([P, 2, P], F32)
         for u in range(2):
             nc.tensor.transpose(x_t[:, u, :], x_words[:, u : HIDDEN // 2 : 2], identity[:])
-        copiers = (nc.vector.tensor_copy, nc.scalar.copy)
         for e in range(ROW_TOKENS):
-            copiers[e](
+            nc.vector.tensor_copy(
                 out=strips[e][:, 0 : 2 * 2 * (P + 2) * 2]
                 .bitcast(F32)
                 .rearrange("p (a y) -> p a y", a=HALVES)[:, :, 0 : 2 * P]
@@ -131,17 +134,17 @@ def tile_attention_pa_s_kernel(
             x_scales.append(planes)
 
         pass_order = []
-        for group in range(UNITS_PER_PART):
-            pass_order.extend([(V_PART, group), (Q_PART, group)])
-        for group in range(UNITS_PER_PART):
-            pass_order.append((K_PART, group))
+        for index, part in enumerate((Q_PART, K_PART)):
+            for octet in range(2):
+                pass_order.extend([(part, 2 * octet), (part, 2 * octet + 1), (V_PART, 2 * index + octet)])
 
         sums = {}
         for part, group in pass_order:
             acc = psum_acc.tile([P, UNIT_COLS], F32)
             for e in range(ROW_TOKENS):
                 for half in (1, 0):
-                    first_col = part * PART_COLS + (group * HALVES + half) * PASS_COLS
+                    first_head = STORE_HEADS * (group // 2) + 4 * half + UNIT_HEADS * (group % 2)
+                    first_col = part * PART_COLS + first_head * HEAD_DIM
                     nc.tensor.matmul_mx(
                         out=acc[:, e * PASS_COLS : (e + 1) * PASS_COLS],
                         lhsT=x_codes[e][:, half * P : (half + 1) * P].bitcast(FP8X4),
@@ -155,23 +158,25 @@ def tile_attention_pa_s_kernel(
                     )
             sums[(part, group)] = acc
 
-        def store(part, group, result):
-            heads = slice(group * HALVES * UNIT_HEADS, (group + 1) * HALVES * UNIT_HEADS)
+        def new_result():
+            result = results.tile([P, STORE_UNITS, UNIT_HEADS, ROW_TOKENS * HEAD_DIM], F32)
+            return result
+
+        def store(part, octet, result):
+            heads = slice(octet * STORE_HEADS, (octet + 1) * STORE_HEADS)
             for b in range(BATCH):
                 nc.sync.dma_start(
                     out=outs[part][b, heads, :, :].rearrange("x (m e) d -> m x (e d)", e=ROW_TOKENS),
-                    in_=result[b:P:BATCH, :, :],
+                    in_=result[b:P:BATCH].rearrange("p q h f -> p (q h) f"),
                 )
 
-        for group in range(UNITS_PER_PART):
-            v_sb = v_work.tile([P, UNIT_HEADS, ROW_TOKENS * HEAD_DIM], F32)
+        def leave(group, result):
             nc.scalar.copy(
-                out=v_sb[:].rearrange("p h (e d) -> p h e d", e=ROW_TOKENS),
+                out=result[:, group % 2].rearrange("p h (e d) -> p h e d", e=ROW_TOKENS),
                 in_=sums[(V_PART, group)][:].rearrange(
                     "p (e h d) -> p h e d", e=ROW_TOKENS, h=UNIT_HEADS
                 ),
             )
-            store(V_PART, group, v_sb)
 
         product_shape = [P, 2, ROW_TOKENS, UNIT_HEADS, PAIRS, 2]
         both_tables = (
@@ -180,8 +185,8 @@ def tile_attention_pa_s_kernel(
             .unsqueeze(3)
             .to_broadcast(product_shape)
         )
-        rope_units = [(part, group) for part in (Q_PART, K_PART) for group in range(UNITS_PER_PART)]
-        for index, (part, group) in enumerate(rope_units):
+
+        def turn(part, group, adder, result):
             elements = (
                 sums[(part, group)][:]
                 .rearrange("p (e h j s) -> p s e h j", e=ROW_TOKENS, h=UNIT_HEADS, s=2)
@@ -190,12 +195,22 @@ def tile_attention_pa_s_kernel(
             )
             products = rope_work.tile(product_shape, F32)
             nc.vector.tensor_tensor(out=products[:], in0=elements, in1=both_tables, op=MULT)
-            adder = nc.gpsimd if index < len(rope_units) - VECTOR_SUMS else nc.vector
-            turned = rope_work.tile([P, UNIT_HEADS, ROW_TOKENS * HEAD_DIM], F32)
             adder.tensor_tensor(
-                out=turned[:].rearrange("p h (e d) -> p h e d", e=ROW_TOKENS),
+                out=result[:, group % 2].rearrange("p h (e d) -> p h e d", e=ROW_TOKENS),
                 in0=products[:, 0].rearrange("p e h j r -> p h e (j r)"),
                 in1=products[:, 1].rearrange("p e h j r -> p h e (j r)"),
                 op=ADD,
             )
-            store(part, group, turned)
+
+        for index, part in enumerate((Q_PART, K_PART)):
+            for octet in range(2):
+                last = part == K_PART and octet == 1
+                turned = new_result()
+                for group in (2 * octet, 2 * octet + 1):
+                    turn(part, group, nc.vector if last else nc.gpsimd, turned)
+                if octet == 0:
+                    v_sb = new_result()
+                    for group in (2 * index, 2 * index + 1):
+                        leave(group, v_sb)
+                    store(V_PART, index, v_sb)
+                store(part, octet, turned)

@@ -31,6 +31,8 @@ WORD_BYTES = 2
 PSUM_BANKS = 8
 VECTOR_SUMS = 2
 PACK = 4
+WARM_BEFORE = 4
+WARM_BETWEEN = 2
 
 FLOPS = 2 * P * HIDDEN * 3 * PART_COLS
 
@@ -48,6 +50,9 @@ def tile_attention_pa_s_kernel(
         results = ctx.enter_context(tc.tile_pool(name="results", bufs=3 * UNITS_PER_PART // STORE_UNITS))
         psum_x = ctx.enter_context(tc.psum_pool(name="psum_x", bufs=1))
         psum_acc = ctx.enter_context(tc.psum_pool(name="psum_acc", bufs=PSUM_BANKS - 1))
+
+        warm = keep.tile([P, P], F32)
+        nc.gpsimd.memset(warm[:], 0.0)
 
         w_scales = keep.tile([P, 3 * PART_COLS], U8, align_bytes=64)
         half_plane = 3 * PART_COLS // 2
@@ -104,12 +109,21 @@ def tile_attention_pa_s_kernel(
             nc.vector.memset(strip[:].bitcast(I32), 0)
             strips.append(strip)
 
+        acc = psum_acc.tile([P, UNIT_COLS], F32)
+        spare = acc
+
+        def idle_passes(count):
+            for index in range(count):
+                nc.tensor.matmul(out=spare[:, 0:P], lhsT=warm[:], rhs=warm[:], start=True, stop=True)
+
+        idle_passes(WARM_BEFORE)
         x_words = x_sb[:].bitcast(F32)
         x_t = psum_x.tile([P, 2, P], F32)
         for u in range(2):
             nc.tensor.transpose(x_t[:, u, :], x_words[:, u : HIDDEN // 2 : 2], identity[:])
+        idle_passes(WARM_BETWEEN)
         for e in range(ROW_TOKENS):
-            nc.vector.tensor_copy(
+            nc.scalar.copy(
                 out=strips[e][:, 0 : 2 * 2 * (P + 2) * 2]
                 .bitcast(F32)
                 .rearrange("p (a y) -> p a y", a=HALVES)[:, :, 0 : 2 * P]

@@ -148,9 +148,9 @@ def tile_attention_pa_s_kernel(
             x_scales.append(planes)
 
         pass_order = []
-        for index, part in enumerate((Q_PART, K_PART)):
-            for octet in range(2):
-                pass_order.extend([(part, 2 * octet), (part, 2 * octet + 1), (V_PART, 2 * index + octet)])
+        for group in range(UNITS_PER_PART):
+            pass_order.extend([(Q_PART, group), (V_PART, group)])
+        pass_order.extend((K_PART, group) for group in range(UNITS_PER_PART))
 
         sums = {}
         for part, group in pass_order:
@@ -216,15 +216,15 @@ def tile_attention_pa_s_kernel(
                 op=ADD,
             )
 
-        for index, part in enumerate((Q_PART, K_PART)):
+        for part in (Q_PART, K_PART):
             for octet in range(2):
                 last = part == K_PART and octet == 1
                 turned = new_result()
                 for group in (2 * octet, 2 * octet + 1):
                     turn(part, group, nc.vector if last else nc.gpsimd, turned)
-                if octet == 0:
+                if part == Q_PART:
                     v_sb = new_result()
-                    for group in (2 * index, 2 * index + 1):
+                    for group in (2 * octet, 2 * octet + 1):
                         leave(group, v_sb)
-                    store(V_PART, index, v_sb)
+                    store(V_PART, octet, v_sb)
                 store(part, octet, turned)

@@ -80,10 +80,10 @@ def tile_attention_pa_s_kernel(
             )
 
         load_words(Q_PART)
-        for quadrant in range(4):
+        for r in range(4):
             nc.sync.dma_start(
-                out=w_scales[32 * quadrant : 32 * quadrant + 4, :].bitcast(I32),
-                in_=qkv_w_scales[0, 4 * quadrant : 4 * quadrant + 4, :].bitcast(I32),
+                out=w_scales[r:P:32, :].bitcast(I32),
+                in_=qkv_w_scales[0, r:16:4, :].bitcast(I32),
             )
         load_words(V_PART)
         load_words(K_PART)

@@ -19,12 +19,12 @@ PAIRS = HEAD_DIM // 2
 ROW_TOKENS = 2
 ROWS = POSITIONS // ROW_TOKENS
 HALVES = 2
-UNIT_HEADS = 2
-PASS_COLS = UNIT_HEADS * HEAD_DIM
-UNIT_COLS = ROW_TOKENS * PASS_COLS
-UNITS_PER_PART = HEADS // (HALVES * UNIT_HEADS)
-STORE_UNITS = 2
-STORE_HEADS = STORE_UNITS * HALVES * UNIT_HEADS
+STORE_HEADS = 8
+HALF_HEADS = STORE_HEADS // HALVES
+OCTETS = HEADS // STORE_HEADS
+PASS_COLS = 128
+UNIT_COLS = HALF_HEADS * HEAD_DIM
+UNITS_PER_PART = OCTETS * ROW_TOKENS
 PART_COLS = HEADS * HEAD_DIM
 Q_PART, K_PART, V_PART = 0, 1, 2
 WORD_BYTES = 2
@@ -32,7 +32,6 @@ PSUM_BANKS = 8
 VECTOR_SUMS = 2
 PACK = 4
 WARM_BEFORE = 4
-WARM_BETWEEN = 2
 
 FLOPS = 2 * P * HIDDEN * 3 * PART_COLS
 
@@ -47,7 +46,7 @@ def tile_attention_pa_s_kernel(
         ctx.enter_context(tc.manual_schedule())
         keep = ctx.enter_context(tc.tile_pool(name="keep", bufs=1))
         rope_work = ctx.enter_context(tc.tile_pool(name="rope_work", bufs=2 * UNITS_PER_PART))
-        results = ctx.enter_context(tc.tile_pool(name="results", bufs=3 * UNITS_PER_PART // STORE_UNITS))
+        results = ctx.enter_context(tc.tile_pool(name="results", bufs=3 * OCTETS))
         psum_x = ctx.enter_context(tc.psum_pool(name="psum_x", bufs=1))
         psum_acc = ctx.enter_context(tc.psum_pool(name="psum_acc", bufs=PSUM_BANKS - 1))
 
@@ -69,6 +68,9 @@ def tile_attention_pa_s_kernel(
                 [ROWS, BATCH * HALVES, ROW_TOKENS * HEAD_DIM]
             ),
         )
+
+        table_load = keep.tile([P, 1], F32)
+        nc.scalar.copy(out=table_load[:], in_=warm[:, 0:1])
 
         w_words = keep.tile([P, 3 * PART_COLS * WORD_BYTES], U8, align_bytes=64)
 
@@ -121,7 +123,6 @@ def tile_attention_pa_s_kernel(
         x_t = psum_x.tile([P, 2, P], F32)
         for u in range(2):
             nc.tensor.transpose(x_t[:, u, :], x_words[:, u : HIDDEN // 2 : 2], identity[:])
-        idle_passes(WARM_BETWEEN)
         for e in range(ROW_TOKENS):
             nc.scalar.copy(
                 out=strips[e][:, 0 : 2 * 2 * (P + 2) * 2]
@@ -147,20 +148,22 @@ def tile_attention_pa_s_kernel(
             x_codes.append(codes)
             x_scales.append(planes)
 
+        positions = [(octet, e) for octet in range(OCTETS) for e in range(ROW_TOKENS)]
         pass_order = []
-        for group in range(UNITS_PER_PART):
-            pass_order.extend([(Q_PART, group), (V_PART, group)])
-        pass_order.extend((K_PART, group) for group in range(UNITS_PER_PART))
+        for octet, e in positions:
+            pass_order.extend([(Q_PART, octet, e), (V_PART, octet, e)])
+        for octet, e in positions:
+            pass_order.append((K_PART, octet, e))
 
         sums = {}
-        for part, group in pass_order:
+        for part, octet, e in pass_order:
             acc = psum_acc.tile([P, UNIT_COLS], F32)
-            for e in range(ROW_TOKENS):
+            for pair in range(UNIT_COLS // PASS_COLS):
                 for half in (1, 0):
-                    first_head = STORE_HEADS * (group // 2) + 4 * half + UNIT_HEADS * (group % 2)
-                    first_col = part * PART_COLS + first_head * HEAD_DIM
+                    first_head = STORE_HEADS * octet + HALF_HEADS * half
+                    first_col = part * PART_COLS + first_head * HEAD_DIM + pair * PASS_COLS
                     nc.tensor.matmul_mx(
-                        out=acc[:, e * PASS_COLS : (e + 1) * PASS_COLS],
+                        out=acc[:, pair * PASS_COLS : (pair + 1) * PASS_COLS],
                         lhsT=x_codes[e][:, half * P : (half + 1) * P].bitcast(FP8X4),
                         lhsT_scale=x_scales[e][:, half * P : (half + 1) * P],
                         rhs=w_words[
@@ -170,10 +173,10 @@ def tile_attention_pa_s_kernel(
                         start=(half == 1),
                         stop=(half == 0),
                     )
-            sums[(part, group)] = acc
+            sums[(part, octet, e)] = acc
 
         def new_result():
-            result = results.tile([P, STORE_UNITS, UNIT_HEADS, ROW_TOKENS * HEAD_DIM], F32)
+            result = results.tile([P, HALF_HEADS, ROW_TOKENS, HEAD_DIM], F32)
             return result
 
         def store(part, octet, result):
@@ -181,50 +184,58 @@ def tile_attention_pa_s_kernel(
             for b in range(BATCH):
                 nc.sync.dma_start(
                     out=outs[part][b, heads, :, :].rearrange("x (m e) d -> m x (e d)", e=ROW_TOKENS),
-                    in_=result[b:P:BATCH].rearrange("p q h f -> p (q h) f"),
+                    in_=result[b:P:BATCH].rearrange("p h e d -> p h (e d)"),
                 )
 
-        def leave(group, result):
+        def leave(octet, e, result):
             nc.scalar.copy(
-                out=result[:, group % 2].rearrange("p h (e d) -> p h e d", e=ROW_TOKENS),
-                in_=sums[(V_PART, group)][:].rearrange(
-                    "p (e h d) -> p h e d", e=ROW_TOKENS, h=UNIT_HEADS
-                ),
+                out=result[:, :, e],
+                in_=sums[(V_PART, octet, e)][:].rearrange("p (h d) -> p h d", h=HALF_HEADS),
             )
 
-        product_shape = [P, 2, ROW_TOKENS, UNIT_HEADS, PAIRS, 2]
-        both_tables = (
-            tables[:]
-            .rearrange("p s e (j r) -> p s e j r", r=2)
-            .unsqueeze(3)
-            .to_broadcast(product_shape)
-        )
+        product_shape = [P, 2, HALF_HEADS, PAIRS, 2]
 
-        def turn(part, group, adder, result):
+        def multiply(part, octet, e):
             elements = (
-                sums[(part, group)][:]
-                .rearrange("p (e h j s) -> p s e h j", e=ROW_TOKENS, h=UNIT_HEADS, s=2)
-                .unsqueeze(5)
+                sums[(part, octet, e)][:]
+                .rearrange("p (h j s) -> p s h j", h=HALF_HEADS, s=2)
+                .unsqueeze(4)
+                .to_broadcast(product_shape)
+            )
+            both_tables = (
+                tables[:, :, e]
+                .rearrange("p s (j r) -> p s j r", r=2)
+                .unsqueeze(2)
                 .to_broadcast(product_shape)
             )
             products = rope_work.tile(product_shape, F32)
             nc.vector.tensor_tensor(out=products[:], in0=elements, in1=both_tables, op=MULT)
+            return products
+
+        def add(adder, products, e, result):
             adder.tensor_tensor(
-                out=result[:, group % 2].rearrange("p h (e d) -> p h e d", e=ROW_TOKENS),
-                in0=products[:, 0].rearrange("p e h j r -> p h e (j r)"),
-                in1=products[:, 1].rearrange("p e h j r -> p h e (j r)"),
+                out=result[:, :, e],
+                in0=products[:, 0].rearrange("p h j r -> p h (j r)"),
+                in1=products[:, 1].rearrange("p h j r -> p h (j r)"),
                 op=ADD,
             )
 
         for part in (Q_PART, K_PART):
-            for octet in range(2):
-                last = part == K_PART and octet == 1
+            for octet in range(OCTETS):
+                last = part == K_PART and octet == OCTETS - 1
                 turned = new_result()
-                for group in (2 * octet, 2 * octet + 1):
-                    turn(part, group, nc.vector if last else nc.gpsimd, turned)
+                pending = []
+                for e in range(ROW_TOKENS):
+                    products = multiply(part, octet, e)
+                    if last:
+                        pending.append(products)
+                    else:
+                        add(nc.gpsimd, products, e, turned)
+                for e in range(len(pending)):
+                    add(nc.vector, pending[e], e, turned)
                 if part == Q_PART:
                     v_sb = new_result()
-                    for group in (2 * octet, 2 * octet + 1):
-                        leave(group, v_sb)
+                    for e in range(ROW_TOKENS):
+                        leave(octet, e, v_sb)
                     store(V_PART, octet, v_sb)
                 store(part, octet, turned)

@@ -32,6 +32,7 @@ PSUM_BANKS = 8
 VECTOR_SUMS = 2
 PACK = 4
 WARM_BEFORE = 4
+WARM_BETWEEN = 2
 
 FLOPS = 2 * P * HIDDEN * 3 * PART_COLS
 
@@ -123,6 +124,7 @@ def tile_attention_pa_s_kernel(
         x_t = psum_x.tile([P, 2, P], F32)
         for u in range(2):
             nc.tensor.transpose(x_t[:, u, :], x_words[:, u : HIDDEN // 2 : 2], identity[:])
+        idle_passes(WARM_BETWEEN)
         for e in range(ROW_TOKENS):
             nc.scalar.copy(
                 out=strips[e][:, 0 : 2 * 2 * (P + 2) * 2]

@@ -55,9 +55,7 @@ def tile_attention_pa_s_kernel(
         nc.gpsimd.memset(warm[:], 0.0)
 
         w_scales = keep.tile([P, 3 * PART_COLS], U8, align_bytes=64)
-        half_plane = 3 * PART_COLS // 2
-        nc.vector.memset(w_scales[:, 0:half_plane].bitcast(I32), 0)
-        nc.gpsimd.memset(w_scales[:, half_plane:].bitcast(F32), 0.0)
+        nc.vector.memset(w_scales[:].bitcast(I32), 0)
 
         x_sb = keep.tile([P, HIDDEN], BF16)
         nc.sync.dma_start(out=x_sb[:], in_=x.rearrange("b n k -> n b k"))
@@ -96,7 +94,16 @@ def tile_attention_pa_s_kernel(
 
         first_pairs = tables[:, 0].rearrange("p e (j r) -> p e j r", r=2)
         second_pairs = tables[:, 1].rearrange("p e (j r) -> p e j r", r=2)
-        nc.gpsimd.tensor_scalar(
+
+        strip_words = HALVES * P * 2
+        strips = keep.tile([P, ROW_TOKENS, strip_words * 2 + 64], BF16, align_bytes=64)
+        words = strips[:].rearrange("p e y -> p (e y)").bitcast(I32).rearrange("p (e y) -> p e y", e=ROW_TOKENS)
+        for half in range(HALVES):
+            first_zero = 2 * P * half + 4 * (1 - half)
+            nc.vector.memset(
+                words[:, :, first_zero : first_zero + 2 * P].rearrange("p e (m r) -> p e m r", r=8)[:, :, :, 0:4], 0
+            )
+        nc.vector.tensor_scalar(
             out=second_pairs[:, :, :, 0:1],
             in0=first_pairs[:, :, :, 1:2],
             scalar1=-1.0,
@@ -104,13 +111,7 @@ def tile_attention_pa_s_kernel(
             op0=MULT,
             op1=ADD,
         )
-        nc.gpsimd.tensor_copy(out=second_pairs[:, :, :, 1:2], in_=first_pairs[:, :, :, 0:1])
-
-        strips = []
-        for e in range(ROW_TOKENS):
-            strip = keep.tile([P, HALVES * P * PACK + 64], BF16, align_bytes=64, name="strip%d" % e)
-            nc.vector.memset(strip[:].bitcast(I32), 0)
-            strips.append(strip)
+        nc.vector.tensor_copy(out=second_pairs[:, :, :, 1:2], in_=first_pairs[:, :, :, 0:1])
 
         acc = psum_acc.tile([P, UNIT_COLS], F32)
         spare = acc
@@ -127,7 +128,7 @@ def tile_attention_pa_s_kernel(
         idle_passes(WARM_BETWEEN)
         for e in range(ROW_TOKENS):
             nc.scalar.copy(
-                out=strips[e][:, 0 : 2 * 2 * (P + 2) * 2]
+                out=strips[:, e, 0 : 2 * 2 * (P + 2) * 2]
                 .bitcast(F32)
                 .rearrange("p (a y) -> p a y", a=HALVES)[:, :, 0 : 2 * P]
                 .rearrange("p a (m r) -> p a m r", r=8)[:, :, :, 0:4]
@@ -145,7 +146,7 @@ def tile_attention_pa_s_kernel(
             nc.vector.quantize_mx(
                 out=codes[:].bitcast(FP8X4),
                 scales=planes[:],
-                in_=strips[e][:, 0 : HALVES * P * PACK],
+                in_=strips[:, e, 0 : HALVES * P * PACK],
             )
             x_codes.append(codes)
             x_scales.append(planes)

@@ -22,14 +22,14 @@ HALVES = 2
 STORE_HEADS = 8
 HALF_HEADS = STORE_HEADS // HALVES
 OCTETS = HEADS // STORE_HEADS
-PASS_COLS = 128
+PASS_HEADS = 2
+PASS_COLS = PASS_HEADS * HEAD_DIM
 UNIT_COLS = HALF_HEADS * HEAD_DIM
 UNITS_PER_PART = OCTETS * ROW_TOKENS
 PART_COLS = HEADS * HEAD_DIM
 Q_PART, K_PART, V_PART = 0, 1, 2
 WORD_BYTES = 2
 PSUM_BANKS = 8
-VECTOR_SUMS = 2
 PACK = 4
 WARM_BEFORE = 4
 WARM_BETWEEN = 2
@@ -155,35 +155,44 @@ def tile_attention_pa_s_kernel(
         pass_order = []
         for octet, e in positions:
             pass_order.extend([(Q_PART, octet, e), (V_PART, octet, e)])
-        for octet, e in positions:
-            pass_order.append((K_PART, octet, e))
+        for e in range(ROW_TOKENS):
+            pass_order.append((K_PART, 0, e))
+
+        def project(acc, acc_pass, part, e, first_heads):
+            for half in (1, 0):
+                first_col = part * PART_COLS + first_heads[half] * HEAD_DIM
+                nc.tensor.matmul_mx(
+                    out=acc[:, acc_pass * PASS_COLS : (acc_pass + 1) * PASS_COLS],
+                    lhsT=x_codes[e][:, half * P : (half + 1) * P].bitcast(FP8X4),
+                    lhsT_scale=x_scales[e][:, half * P : (half + 1) * P],
+                    rhs=w_words[
+                        :, first_col * WORD_BYTES : (first_col + PASS_COLS) * WORD_BYTES
+                    ].bitcast(FP4X4),
+                    rhs_scale=w_scales[:, first_col : first_col + PASS_COLS],
+                    start=(half == 1),
+                    stop=(half == 0),
+                )
 
         sums = {}
         for part, octet, e in pass_order:
             acc = psum_acc.tile([P, UNIT_COLS], F32)
             for pair in range(UNIT_COLS // PASS_COLS):
-                for half in (1, 0):
-                    first_head = STORE_HEADS * octet + HALF_HEADS * half
-                    first_col = part * PART_COLS + first_head * HEAD_DIM + pair * PASS_COLS
-                    nc.tensor.matmul_mx(
-                        out=acc[:, pair * PASS_COLS : (pair + 1) * PASS_COLS],
-                        lhsT=x_codes[e][:, half * P : (half + 1) * P].bitcast(FP8X4),
-                        lhsT_scale=x_scales[e][:, half * P : (half + 1) * P],
-                        rhs=w_words[
-                            :, first_col * WORD_BYTES : (first_col + PASS_COLS) * WORD_BYTES
-                        ].bitcast(FP4X4),
-                        rhs_scale=w_scales[:, first_col : first_col + PASS_COLS],
-                        start=(half == 1),
-                        stop=(half == 0),
-                    )
+                first_head = STORE_HEADS * octet + PASS_HEADS * pair
+                project(acc, pair, part, e, (first_head, first_head + HALF_HEADS))
             sums[(part, octet, e)] = acc
+        last_sums = []
+        for quad in range(2):
+            acc = psum_acc.tile([P, UNIT_COLS], F32)
+            first_head = HEADS - STORE_HEADS + 2 * PASS_HEADS * quad
+            for e in range(ROW_TOKENS):
+                project(acc, e, K_PART, e, (first_head, first_head + PASS_HEADS))
+            last_sums.append(acc)
 
         def new_result():
             result = results.tile([P, HALF_HEADS, ROW_TOKENS, HEAD_DIM], F32)
             return result
 
-        def store(part, octet, result):
-            heads = slice(octet * STORE_HEADS, (octet + 1) * STORE_HEADS)
+        def store(part, heads, result):
             for b in range(BATCH):
                 nc.sync.dma_start(
                     out=outs[part][b, heads, :, :].rearrange("x (m e) d -> m x (e d)", e=ROW_TOKENS),
@@ -223,22 +232,48 @@ def tile_attention_pa_s_kernel(
                 op=ADD,
             )
 
-        for part in (Q_PART, K_PART):
-            for octet in range(OCTETS):
-                last = part == K_PART and octet == OCTETS - 1
-                turned = new_result()
-                pending = []
-                for e in range(ROW_TOKENS):
-                    products = multiply(part, octet, e)
-                    if last:
-                        pending.append(products)
-                    else:
-                        add(nc.gpsimd, products, e, turned)
-                for e in range(len(pending)):
-                    add(nc.vector, pending[e], e, turned)
-                if part == Q_PART:
-                    v_sb = new_result()
-                    for e in range(ROW_TOKENS):
-                        leave(octet, e, v_sb)
-                    store(V_PART, octet, v_sb)
-                store(part, octet, turned)
+        def octet_heads(octet):
+            return slice(octet * STORE_HEADS, (octet + 1) * STORE_HEADS)
+
+        for part, octet in ((Q_PART, 0), (Q_PART, 1)):
+            turned = new_result()
+            for e in range(ROW_TOKENS):
+                add(nc.gpsimd, multiply(part, octet, e), e, turned)
+            v_sb = new_result()
+            for e in range(ROW_TOKENS):
+                leave(octet, e, v_sb)
+            store(V_PART, octet_heads(octet), v_sb)
+            store(part, octet_heads(octet), turned)
+
+        turned = new_result()
+        add(nc.gpsimd, multiply(K_PART, 0, 0), 0, turned)
+        late = multiply(K_PART, 0, 1)
+        quad_shape = [P, 2, ROW_TOKENS, PASS_HEADS, PAIRS, 2]
+        last_products = []
+        for acc in last_sums:
+            products = rope_work.tile(quad_shape, F32)
+            nc.vector.tensor_tensor(
+                out=products[:],
+                in0=acc[:]
+                .rearrange("p (e h j s) -> p s e h j", e=ROW_TOKENS, h=PASS_HEADS, s=2)
+                .unsqueeze(5)
+                .to_broadcast(quad_shape),
+                in1=tables[:]
+                .rearrange("p s e (j r) -> p s e j r", r=2)
+                .unsqueeze(3)
+                .to_broadcast(quad_shape),
+                op=MULT,
+            )
+            last_products.append(products)
+        add(nc.vector, late, 1, turned)
+        store(K_PART, octet_heads(0), turned)
+        for quad in range(2):
+            result = results.tile([P, PASS_HEADS, ROW_TOKENS, HEAD_DIM], F32, name="last_result", bufs=2)
+            nc.vector.tensor_tensor(
+                out=result[:],
+                in0=last_products[quad][:, 0].rearrange("p e h j r -> p h e (j r)"),
+                in1=last_products[quad][:, 1].rearrange("p e h j r -> p h e (j r)"),
+                op=ADD,
+            )
+            first_head = HEADS - STORE_HEADS + 2 * PASS_HEADS * quad
+            store(K_PART, slice(first_head, first_head + 2 * PASS_HEADS), result)

@@ -151,10 +151,10 @@ def tile_attention_pa_s_kernel(
             x_codes.append(codes)
             x_scales.append(planes)
 
-        positions = [(octet, e) for octet in range(OCTETS) for e in range(ROW_TOKENS)]
         pass_order = []
-        for octet, e in positions:
-            pass_order.extend([(Q_PART, octet, e), (V_PART, octet, e)])
+        for octet in range(OCTETS):
+            for part in (Q_PART, V_PART):
+                pass_order.extend([(part, octet, e) for e in range(ROW_TOKENS)])
         for e in range(ROW_TOKENS):
             pass_order.append((K_PART, 0, e))
 

@@ -31,7 +31,7 @@ Q_PART, K_PART, V_PART = 0, 1, 2
 WORD_BYTES = 2
 PSUM_BANKS = 8
 PACK = 4
-WARM_BEFORE = 4
+WARM_BEFORE = 3
 WARM_BETWEEN = 2
 
 FLOPS = 2 * P * HIDDEN * 3 * PART_COLS

@@ -73,21 +73,22 @@ def tile_attention_pa_s_kernel(
 
         w_words = keep.tile([P, 3 * PART_COLS * WORD_BYTES], U8, align_bytes=64)
 
-        def load_words(part):
-            byte_cols = slice(part * PART_COLS * WORD_BYTES, (part + 1) * PART_COLS * WORD_BYTES)
+        def load_words(first_col, last_col):
+            byte_cols = slice(first_col * WORD_BYTES, last_col * WORD_BYTES)
             nc.sync.dma_start(
                 out=w_words[:, byte_cols].bitcast(I32),
                 in_=qkv_w_words[0, :, byte_cols].bitcast(I32),
             )
 
-        load_words(Q_PART)
+        octet_cols = STORE_HEADS * HEAD_DIM
+        load_words(0, octet_cols)
         for r in range(4):
             nc.sync.dma_start(
                 out=w_scales[r:P:32, :].bitcast(I32),
                 in_=qkv_w_scales[0, r:16:4, :].bitcast(I32),
             )
-        load_words(V_PART)
-        load_words(K_PART)
+        load_words(V_PART * PART_COLS, 3 * PART_COLS)
+        load_words(octet_cols, V_PART * PART_COLS)
 
         identity = keep.tile([P, P], F32)
         masks.make_identity(nc, identity[:])

from contextlib import ExitStack

import concourse.masks as masks
import concourse.mybir as mybir

F32 = mybir.dt.float32
BF16 = mybir.dt.bfloat16
I32 = mybir.dt.int32
U32 = mybir.dt.uint32
U8 = mybir.dt.uint8
FP8X4 = mybir.dt.float8_e4m3fn_x4
FP4X4 = mybir.dt.float4_e2m1fn_x4
MULT = mybir.AluOpType.mult
ADD = mybir.AluOpType.add

BATCH, POSITIONS, HIDDEN, HEADS, HEAD_DIM = 2, 64, 512, 16, 64
P = 128
PAIRS = HEAD_DIM // 2
ROW_TOKENS = 2
ROWS = POSITIONS // ROW_TOKENS
HALVES = 2
STORE_HEADS = 8
HALF_HEADS = STORE_HEADS // HALVES
OCTETS = HEADS // STORE_HEADS
PASS_HEADS = 2
PASS_COLS = PASS_HEADS * HEAD_DIM
UNIT_COLS = HALF_HEADS * HEAD_DIM
UNITS_PER_PART = OCTETS * ROW_TOKENS
PART_COLS = HEADS * HEAD_DIM
Q_PART, K_PART, V_PART = 0, 1, 2
WORD_BYTES = 2
PSUM_BANKS = 8
PACK = 4
WARM_BEFORE = 3
WARM_BETWEEN = 2

FLOPS = 2 * P * HIDDEN * 3 * PART_COLS


def tile_attention_pa_s_kernel(
    tc, x, rope, qkv_w_words, qkv_w_scales, out_0, out_1, out_2
):
    nc = tc.nc
    outs = (out_0, out_1, out_2)

    with ExitStack() as ctx:
        ctx.enter_context(tc.manual_schedule())
        keep = ctx.enter_context(tc.tile_pool(name="keep", bufs=1))
        rope_work = ctx.enter_context(tc.tile_pool(name="rope_work", bufs=2 * UNITS_PER_PART))
        results = ctx.enter_context(tc.tile_pool(name="results", bufs=3 * OCTETS))
        psum_x = ctx.enter_context(tc.psum_pool(name="psum_x", bufs=1))
        psum_acc = ctx.enter_context(tc.psum_pool(name="psum_acc", bufs=PSUM_BANKS - 1))

        warm = keep.tile([P, P], F32)
        nc.gpsimd.memset(warm[:], 0.0)

        w_scales = keep.tile([P, 3 * PART_COLS], U8, align_bytes=64)
        nc.vector.memset(w_scales[:].bitcast(I32), 0)

        x_sb = keep.tile([P, HIDDEN], BF16)
        nc.sync.dma_start(out=x_sb[:], in_=x.rearrange("b n k -> n b k"))

        tables = keep.tile([P, 2, ROW_TOKENS, HEAD_DIM], BF16)
        nc.scalar.dma_start(
            out=tables[:, 0].rearrange("p e d -> p (e d)"),
            in_=rope.rearrange("(m e) o d -> m o (e d)", e=ROW_TOKENS).to_broadcast(
                [ROWS, BATCH * HALVES, ROW_TOKENS * HEAD_DIM]
            ),
        )

        table_load = keep.tile([P, 1], F32)
        nc.scalar.copy(out=table_load[:], in_=warm[:, 0:1])

        w_words = keep.tile([P, 3 * PART_COLS * WORD_BYTES], U8, align_bytes=64)

        def load_words(first_col, last_col):
            byte_cols = slice(first_col * WORD_BYTES, last_col * WORD_BYTES)
            nc.sync.dma_start(
                out=w_words[:, byte_cols].bitcast(I32),
                in_=qkv_w_words[0, :, byte_cols].bitcast(I32),
            )

        octet_cols = STORE_HEADS * HEAD_DIM
        load_words(0, octet_cols)
        for r in range(4):
            nc.sync.dma_start(
                out=w_scales[r:P:32, :].bitcast(I32),
                in_=qkv_w_scales[0, r:16:4, :].bitcast(I32),
            )
        load_words(V_PART * PART_COLS, 3 * PART_COLS)
        load_words(octet_cols, V_PART * PART_COLS)

        identity = keep.tile([P, P], F32)
        masks.make_identity(nc, identity[:])

        first_pairs = tables[:, 0].rearrange("p e (j r) -> p e j r", r=2)
        second_pairs = tables[:, 1].rearrange("p e (j r) -> p e j r", r=2)

        strip_words = HALVES * P * 2
        strips = keep.tile([P, ROW_TOKENS, strip_words * 2 + 64], BF16, align_bytes=64)
        words = strips[:].rearrange("p e y -> p (e y)").bitcast(I32).rearrange("p (e y) -> p e y", e=ROW_TOKENS)
        for half in range(HALVES):
            first_zero = 2 * P * half + 4 * (1 - half)
            nc.vector.memset(
                words[:, :, first_zero : first_zero + 2 * P].rearrange("p e (m r) -> p e m r", r=8)[:, :, :, 0:4], 0
            )
        nc.vector.tensor_scalar(
            out=second_pairs[:, :, :, 0:1],
            in0=first_pairs[:, :, :, 1:2],
            scalar1=-1.0,
            scalar2=0.0,
            op0=MULT,
            op1=ADD,
        )
        nc.vector.tensor_copy(out=second_pairs[:, :, :, 1:2], in_=first_pairs[:, :, :, 0:1])

        acc = psum_acc.tile([P, UNIT_COLS], F32)
        spare = acc

        def idle_passes(count):
            for index in range(count):
                nc.tensor.matmul(out=spare[:, 0:P], lhsT=warm[:], rhs=warm[:], start=True, stop=True)

        idle_passes(WARM_BEFORE)
        x_words = x_sb[:].bitcast(F32)
        x_t = psum_x.tile([P, 2, P], F32)
        for u in range(2):
            nc.tensor.transpose(x_t[:, u, :], x_words[:, u : HIDDEN // 2 : 2], identity[:])
        idle_passes(WARM_BETWEEN)
        for e in range(ROW_TOKENS):
            nc.scalar.copy(
                out=strips[:, e, 0 : 2 * 2 * (P + 2) * 2]
                .bitcast(F32)
                .rearrange("p (a y) -> p a y", a=HALVES)[:, :, 0 : 2 * P]
                .rearrange("p a (m r) -> p a m r", r=8)[:, :, :, 0:4]
                .rearrange("p a m (b u) -> p a m b u", u=2),
                in_=x_t[:]
                .rearrange("p u (m e b) -> p e m b u", e=2, b=2)[:, e]
                .unsqueeze(1)
                .to_broadcast([P, HALVES, ROWS, 2, 2]),
            )
        x_codes = []
        x_scales = []
        for e in range(ROW_TOKENS):
            codes = keep.tile([P, HALVES * P], U32, align_bytes=64, name="codes%d" % e)
            planes = keep.tile([P, HALVES * P], U8, align_bytes=64, name="planes%d" % e)
            nc.vector.quantize_mx(
                out=codes[:].bitcast(FP8X4),
                scales=planes[:],
                in_=strips[:, e, 0 : HALVES * P * PACK],
            )
            x_codes.append(codes)
            x_scales.append(planes)

        pass_order = []
        for octet in range(OCTETS):
            for part in (Q_PART, V_PART):
                pass_order.extend([(part, octet, e) for e in range(ROW_TOKENS)])
        for e in range(ROW_TOKENS):
            pass_order.append((K_PART, 0, e))

        def project(acc, acc_pass, part, e, first_heads):
            for half in (1, 0):
                first_col = part * PART_COLS + first_heads[half] * HEAD_DIM
                nc.tensor.matmul_mx(
                    out=acc[:, acc_pass * PASS_COLS : (acc_pass + 1) * PASS_COLS],
                    lhsT=x_codes[e][:, half * P : (half + 1) * P].bitcast(FP8X4),
                    lhsT_scale=x_scales[e][:, half * P : (half + 1) * P],
                    rhs=w_words[
                        :, first_col * WORD_BYTES : (first_col + PASS_COLS) * WORD_BYTES
                    ].bitcast(FP4X4),
                    rhs_scale=w_scales[:, first_col : first_col + PASS_COLS],
                    start=(half == 1),
                    stop=(half == 0),
                )

        sums = {}
        for part, octet, e in pass_order:
            acc = psum_acc.tile([P, UNIT_COLS], F32)
            for pair in range(UNIT_COLS // PASS_COLS):
                first_head = STORE_HEADS * octet + PASS_HEADS * pair
                project(acc, pair, part, e, (first_head, first_head + HALF_HEADS))
            sums[(part, octet, e)] = acc
        last_sums = []
        for quad in range(2):
            acc = psum_acc.tile([P, UNIT_COLS], F32)
            first_head = HEADS - STORE_HEADS + 2 * PASS_HEADS * quad
            for e in range(ROW_TOKENS):
                project(acc, e, K_PART, e, (first_head, first_head + PASS_HEADS))
            last_sums.append(acc)

        def new_result():
            result = results.tile([P, HALF_HEADS, ROW_TOKENS, HEAD_DIM], F32)
            return result

        def store(part, heads, result):
            for b in range(BATCH):
                nc.sync.dma_start(
                    out=outs[part][b, heads, :, :].rearrange("x (m e) d -> m x (e d)", e=ROW_TOKENS),
                    in_=result[b:P:BATCH].rearrange("p h e d -> p h (e d)"),
                )

        def leave(octet, e, result):
            nc.scalar.copy(
                out=result[:, :, e],
                in_=sums[(V_PART, octet, e)][:].rearrange("p (h d) -> p h d", h=HALF_HEADS),
            )

        product_shape = [P, 2, HALF_HEADS, PAIRS, 2]

        def multiply(part, octet, e):
            elements = (
                sums[(part, octet, e)][:]
                .rearrange("p (h j s) -> p s h j", h=HALF_HEADS, s=2)
                .unsqueeze(4)
                .to_broadcast(product_shape)
            )
            both_tables = (
                tables[:, :, e]
                .rearrange("p s (j r) -> p s j r", r=2)
                .unsqueeze(2)
                .to_broadcast(product_shape)
            )
            products = rope_work.tile(product_shape, F32)
            nc.vector.tensor_tensor(out=products[:], in0=elements, in1=both_tables, op=MULT)
            return products

        def add(adder, products, e, result):
            adder.tensor_tensor(
                out=result[:, :, e],
                in0=products[:, 0].rearrange("p h j r -> p h (j r)"),
                in1=products[:, 1].rearrange("p h j r -> p h (j r)"),
                op=ADD,
            )

        def octet_heads(octet):
            return slice(octet * STORE_HEADS, (octet + 1) * STORE_HEADS)

        for part, octet in ((Q_PART, 0), (Q_PART, 1)):
            turned = new_result()
            for e in range(ROW_TOKENS):
                add(nc.gpsimd, multiply(part, octet, e), e, turned)
            v_sb = new_result()
            for e in range(ROW_TOKENS):
                leave(octet, e, v_sb)
            store(V_PART, octet_heads(octet), v_sb)
            store(part, octet_heads(octet), turned)

        turned = new_result()
        add(nc.gpsimd, multiply(K_PART, 0, 0), 0, turned)
        late = multiply(K_PART, 0, 1)
        quad_shape = [P, 2, ROW_TOKENS, PASS_HEADS, PAIRS, 2]
        last_products = []
        for acc in last_sums:
            products = rope_work.tile(quad_shape, F32)
            nc.vector.tensor_tensor(
                out=products[:],
                in0=acc[:]
                .rearrange("p (e h j s) -> p s e h j", e=ROW_TOKENS, h=PASS_HEADS, s=2)
                .unsqueeze(5)
                .to_broadcast(quad_shape),
                in1=tables[:]
                .rearrange("p s e (j r) -> p s e j r", r=2)
                .unsqueeze(3)
                .to_broadcast(quad_shape),
                op=MULT,
            )
            last_products.append(products)
        add(nc.vector, late, 1, turned)
        store(K_PART, octet_heads(0), turned)
        for quad in range(2):
            result = results.tile([P, PASS_HEADS, ROW_TOKENS, HEAD_DIM], F32, name="last_result", bufs=2)
            nc.vector.tensor_tensor(
                out=result[:],
                in0=last_products[quad][:, 0].rearrange("p e h j r -> p h e (j r)"),
                in1=last_products[quad][:, 1].rearrange("p e h j r -> p h e (j r)"),
                op=ADD,
            )
            first_head = HEADS - STORE_HEADS + 2 * PASS_HEADS * quad
            store(K_PART, slice(first_head, first_head + 2 * PASS_HEADS), result)
